import numpy as np
import ml_dtypes


def mxq(x, axis, fmt="e4m3"):
    dtype, down = {"e4m3": (ml_dtypes.float8_e4m3fn, 7), "e5m2": (ml_dtypes.float8_e5m2, 14)}[fmt]
    v = np.moveaxis(np.asarray(x, np.float32).astype(ml_dtypes.bfloat16).astype(np.float64), axis, -1)
    blocks = v.reshape(v.shape[:-1] + (-1, 32))
    amax = np.abs(blocks).max(-1, keepdims=True)
    byte = np.maximum(np.where(amax > 0, np.frexp(amax)[1] - 1 + 127, 0) - down, 1)
    scale = np.exp2(byte - 127.0)
    codes = (blocks / scale).astype(np.float32).astype(dtype).astype(np.float64)
    return np.moveaxis((codes * scale).reshape(v.shape), -1, axis)


WIDE = False


def mx_kscale(k):
    if not WIDE:
        return np.ones(k)
    levels = np.array([10, -10, 5, -5, 0])
    a = np.random.permutation(np.resize(levels, k // 512 * 4)).reshape(k // 512, 4)
    idx = np.arange(k)
    return np.exp2(a[idx // 512, idx % 128 // 32])


BF16 = ml_dtypes.bfloat16


def bf(x):
    return np.asarray(x, np.float32).astype(BF16)


def f64(x):
    return np.asarray(x).astype(np.float64)


B, S, D_IN, D_OUT, R = 4, 2048, 1024, 512, 128
LORA_SCALE = 2.0


def setup_inputs():
    s = mx_kscale(D_IN)
    return {"x": bf(np.random.standard_normal((B, S, D_IN)) * s),
            "weight": bf(np.random.standard_normal((D_OUT, D_IN)) * 1.0 / np.sqrt(D_IN) / s),
            "bias": bf(np.random.standard_normal(D_OUT) * 0.5),
            "lora_left": bf(np.random.standard_normal((D_OUT, R)) * 0.5 / np.sqrt(R)),
            "lora_right": bf(np.random.standard_normal((R, D_IN)) * 0.5 / np.sqrt(D_IN) / s)}


def reference(x, weight, bias, lora_left, lora_right):
    w_eff = f64(weight) + LORA_SCALE * (f64(lora_left) @ f64(lora_right))
    return (mxq(f64(x), 2, "e4m3") @ mxq(w_eff, 1, "e4m3").T) + f64(bias)

@@ -1,0 +1,189 @@
+from contextlib import ExitStack
+
+import concourse.masks as masks
+import concourse.mybir as mybir
+
+F32 = mybir.dt.float32
+BF16 = mybir.dt.bfloat16
+U32 = mybir.dt.uint32
+U8 = mybir.dt.uint8
+FP8X4 = mybir.dt.float8_e4m3fn_x4
+ADD = mybir.AluOpType.add
+
+P = 128
+ROWS = 8192
+D_IN = 1024
+D_OUT = 512
+RANK = 128
+LORA_SCALE = 2.0
+J = 8
+SLABS = ROWS // (P * J)
+UNITS = 2 * SLABS
+FLOPS = 2 * ROWS * D_IN * D_OUT + 2 * D_OUT * RANK * D_IN
+
+
+def tile_loralinear_t_kernel(tc, x, weight, bias, lora_left, lora_right, out):
+    nc = tc.nc
+    xv = x.flatten_outer_dims().rearrange("(s p j) k -> s p (j k)", p=P, j=J)
+    ov = out.flatten_outer_dims().rearrange("(s p j) o -> s p (j o)", p=P, j=J)
+    with ExitStack() as ctx:
+        const = ctx.enter_context(tc.tile_pool(name="const", bufs=1))
+        slabs = ctx.enter_context(tc.tile_pool(name="slabs", bufs=9))
+        work = ctx.enter_context(tc.tile_pool(name="work", bufs=3))
+        ps_t = ctx.enter_context(tc.psum_pool(name="ps_t", bufs=4))
+        ps_o = ctx.enter_context(tc.psum_pool(name="ps_o", bufs=4))
+        ctx.enter_context(tc.manual_schedule())
+
+        ident_bf = const.tile([P, P], BF16, name="ident_bf")
+        masks.make_identity(nc, ident_bf[:])
+        ident_f = const.tile([P, P], F32, name="ident_f")
+        masks.make_identity(nc, ident_f[:])
+        ones = const.tile([P, P], BF16, name="ones")
+        nc.vector.memset(ones[:], 1.0)
+        bias_row = const.tile([P, D_OUT], BF16, name="bias_row")
+        nc.vector.memset(bias_row[:], 0.0)
+
+        ll_sb = const.tile([P, 4, RANK], BF16, name="ll_sb")
+        nc.sync.dma_start(out=ll_sb[:], in_=lora_left.rearrange("(t p) r -> p t r", p=P))
+        lr_sb = const.tile([P, D_IN], BF16, name="lr_sb")
+        nc.sync.dma_start(out=lr_sb[:], in_=lora_right)
+        nc.sync.dma_start(out=bias_row[0:1, :], in_=bias.unsqueeze(0))
+        w_sb = const.tile([P, 2, 4, 512], BF16, name="w_sb")
+        w_dram = weight.rearrange("(t p) (g k) -> g p t k", p=P, g=2)
+        x_tiles = []
+        for s in range(SLABS):
+            x_slab = slabs.tile([P, J * D_IN], BF16, name="x_slab", tag="slab")
+            x_tiles.append(x_slab)
+        half = J * D_IN // 2
+        nc.sync.dma_start(out=w_sb[:, 0], in_=w_dram[0])
+        nc.sync.dma_start(out=x_tiles[0][:, 0:half], in_=xv[0][:, 0:half])
+        nc.sync.dma_start(out=w_sb[:, 1], in_=w_dram[1])
+        nc.sync.dma_start(out=x_tiles[0][:, half : 2 * half], in_=xv[0][:, half : 2 * half])
+        for s in range(1, SLABS):
+            nc.sync.dma_start(out=x_tiles[s][:], in_=xv[s])
+
+        pl = ps_t.tile([P, 4, P], BF16, name="pl", tag="T")
+        for t in range(4):
+            nc.tensor.transpose(pl[:, t, :], ll_sb[:, t, :], ident_bf[:])
+        ll_t2 = const.tile([P, D_OUT], BF16, name="ll_t2")
+        nc.vector.tensor_scalar_mul(out=ll_t2[:], in0=pl[:].rearrange("p t o -> p (t o)"), scalar1=LORA_SCALE)
+
+        pb = ps_t.tile([P, D_OUT], F32, name="pb", tag="T")
+        nc.tensor.matmul(pb[:], lhsT=ones[:], rhs=bias_row[:], start=True, stop=True)
+        bias_sb = const.tile([P, D_OUT], F32, name="bias_sb")
+        nc.scalar.copy(out=bias_sb[:], in_=pb[:])
+
+        w_view = w_sb[:].rearrange("p g t (u q e) -> p g t u q e", u=2, q=P, e=2)
+        lr_view = lr_sb[:].rearrange("p (g u q e) -> p g u q e", g=2, u=2, q=P, e=2)
+        wg = const.tile([P, 2, D_OUT, 4], BF16, name="wg", align_bytes=64)
+        wc = const.tile([P, 2 * D_OUT], U32, name="wc", align_bytes=64)
+        ws = const.tile([P, 2 * D_OUT], U8, name="ws", align_bytes=64)
+
+        def weight_bank(g, t, on_vector):
+            pw = ps_o.tile([P, 4, P], F32, name="pw", tag="O")
+            for v in range(4):
+                u, e = divmod(v, 2)
+                nc.tensor.matmul(pw[:, v, :], lhsT=w_view[:, g, t, u, :, e], rhs=ident_bf[:], start=True, stop=False)
+                nc.tensor.matmul(
+                    pw[:, v, :], lhsT=lr_view[:, g, u, :, e], rhs=ll_t2[:, t * P : (t + 1) * P], start=False, stop=True
+                )
+            dst = wg[:, g, t * P : (t + 1) * P, :]
+            src = pw[:].rearrange("p v o -> p o v")
+            if on_vector:
+                nc.vector.tensor_copy(out=dst, in_=src)
+            else:
+                nc.scalar.copy(out=dst, in_=src)
+
+        def weight_quantise(g):
+            cols = slice(g * D_OUT, (g + 1) * D_OUT)
+            nc.vector.quantize_mx(
+                out=wc[:, cols].bitcast(FP8X4), scales=ws[:, cols], in_=wg[:, g].rearrange("p o v -> p (o v)")
+            )
+
+        groups = {}
+        codes = {}
+        o_tiles = {}
+
+        def transposes(n):
+            s, h = divmod(n, 2)
+            xw = x_tiles[s][:].bitcast(F32)
+            grp = work.tile([P, 4096], BF16, name="grp", tag="grp", align_bytes=64)
+            gw = grp[:].bitcast(F32).rearrange("p (i g r u) -> p i g r u", i=4, g=2, r=P, u=2)
+            for i in range(4):
+                base = (4 * h + i) * 512
+                tb = ps_t.tile([P, 4, P], F32, name="tb", tag="T")
+                for c in range(4):
+                    nc.tensor.transpose(tb[:, c, :], xw[:, base + c * P : base + (c + 1) * P], ident_f[:])
+                nc.scalar.copy(out=gw[:, i], in_=tb[:].rearrange("p (g u) r -> p g r u", u=2))
+            groups[n] = grp
+
+        def quantise(n, part):
+            if part == 0:
+                xc = work.tile([P, 1024], U32, name="xc", tag="xc", align_bytes=64)
+                xs = work.tile([P, 1024], U8, name="xs", tag="xs", align_bytes=64)
+                codes[n] = (xc, xs)
+            xc, xs = codes[n]
+            cols = slice(part * 512, (part + 1) * 512)
+            nc.vector.quantize_mx(
+                out=xc[:, cols].bitcast(FP8X4), scales=xs[:, cols], in_=groups[n][:, part * 2048 : (part + 1) * 2048]
+            )
+
+        def passes(n, i):
+            s, h = divmod(n, 2)
+            if h == 0 and i == 0:
+                o_slab = slabs.tile([P, J * D_OUT], F32, name="o_slab", tag="slab")
+                o_tiles[s] = o_slab
+            xc, xs = codes[n]
+            ob = ps_o.tile([P, D_OUT], F32, name="ob", tag="O")
+            for g in range(2):
+                m_cols = slice((2 * i + g) * P, (2 * i + g + 1) * P)
+                n_cols = slice(g * D_OUT, (g + 1) * D_OUT)
+                nc.tensor.matmul_mx(
+                    out=ob[:],
+                    lhsT=xc[:, m_cols].bitcast(FP8X4),
+                    lhsT_scale=xs[:, m_cols],
+                    rhs=wc[:, n_cols].bitcast(FP8X4),
+                    rhs_scale=ws[:, n_cols],
+                    start=(g == 0),
+                    stop=(g == 1),
+                )
+            j = 4 * h + i
+            nc.vector.tensor_tensor(out=o_tiles[s][:, j * D_OUT : (j + 1) * D_OUT], in0=ob[:], in1=bias_sb[:], op=ADD)
+
+        def store(s, j0, j1):
+            nc.sync.dma_start(out=ov[s][:, j0 * D_OUT : j1 * D_OUT], in_=o_tiles[s][:, j0 * D_OUT : j1 * D_OUT])
+
+        for t in range(4):
+            weight_bank(0, t, True)
+        weight_quantise(0)
+        transposes(0)
+        weight_bank(1, 0, True)
+        weight_bank(1, 1, True)
+        weight_bank(1, 2, False)
+        weight_bank(1, 3, False)
+        quantise(0, 0)
+        quantise(0, 1)
+        weight_quantise(1)
+        transposes(1)
+
+        for n in range(UNITS):
+            s, h = divmod(n, 2)
+            last = s == SLABS - 1
+            if n + 1 < UNITS:
+                quantise(n + 1, 0)
+            passes(n, 0)
+            if n + 1 < UNITS:
+                quantise(n + 1, 1)
+            passes(n, 1)
+            if last and h == 1:
+                store(s, 4, 6)
+            passes(n, 2)
+            passes(n, 3)
+            if last and h == 0:
+                store(s, 0, 4)
+            elif last:
+                store(s, 6, 8)
+            elif h == 1:
+                store(s, 0, 8)
+            if n + 2 < UNITS:
+                transposes(n + 2)

@@ -18,7 +18,8 @@ RANK = 128
 LORA_SCALE = 2.0
 J = 8
 SLABS = ROWS // (P * J)
-UNITS = 2 * SLABS
+BUNCH_SIZES = [2] * 32
+MAX_BUNCH = 2
 FLOPS = 2 * ROWS * D_IN * D_OUT + 2 * D_OUT * RANK * D_IN
 
 
@@ -29,7 +30,7 @@ def tile_loralinear_t_kernel(tc, x, weight, bias, lora_left, lora_right, out):
     with ExitStack() as ctx:
         const = ctx.enter_context(tc.tile_pool(name="const", bufs=1))
         slabs = ctx.enter_context(tc.tile_pool(name="slabs", bufs=9))
-        work = ctx.enter_context(tc.tile_pool(name="work", bufs=3))
+        work = ctx.enter_context(tc.tile_pool(name="work", bufs=4))
         ps_t = ctx.enter_context(tc.psum_pool(name="ps_t", bufs=4))
         ps_o = ctx.enter_context(tc.psum_pool(name="ps_o", bufs=4))
         ctx.enter_context(tc.manual_schedule())
@@ -100,40 +101,55 @@ def tile_loralinear_t_kernel(tc, x, weight, bias, lora_left, lora_right, out):
                 out=wc[:, cols].bitcast(FP8X4), scales=ws[:, cols], in_=wg[:, g].rearrange("p o v -> p (o v)")
             )
 
+        bunches = []
+        first = 0
+        for size in BUNCH_SIZES:
+            bunches.append(list(range(first, first + size)))
+            first += size
+        assert first == ROWS // P
         groups = {}
         codes = {}
         o_tiles = {}
 
-        def transposes(n):
-            s, h = divmod(n, 2)
-            xw = x_tiles[s][:].bitcast(F32)
-            grp = work.tile([P, 4096], BF16, name="grp", tag="grp", align_bytes=64)
-            gw = grp[:].bitcast(F32).rearrange("p (i g r u) -> p i g r u", i=4, g=2, r=P, u=2)
-            for i in range(4):
-                base = (4 * h + i) * 512
+        def transposes(b):
+            tiles = bunches[b]
+            grp = work.tile([P, MAX_BUNCH * 1024], BF16, name="grp", tag="grp", align_bytes=64)
+            gw = grp[:].bitcast(F32).rearrange("p (i g r u) -> p i g r u", i=MAX_BUNCH, g=2, r=P, u=2)
+            for i, rt in enumerate(tiles):
+                s, j = divmod(rt, J)
+                xw = x_tiles[s][:].bitcast(F32)
                 tb = ps_t.tile([P, 4, P], F32, name="tb", tag="T")
                 for c in range(4):
-                    nc.tensor.transpose(tb[:, c, :], xw[:, base + c * P : base + (c + 1) * P], ident_f[:])
+                    nc.tensor.transpose(tb[:, c, :], xw[:, j * 512 + c * P : j * 512 + (c + 1) * P], ident_f[:])
                 nc.scalar.copy(out=gw[:, i], in_=tb[:].rearrange("p (g u) r -> p g r u", u=2))
-            groups[n] = grp
+            groups[b] = grp
+            xc = work.tile([P, MAX_BUNCH * 256], U32, name="xc", tag="xc", align_bytes=64)
+            xs = work.tile([P, MAX_BUNCH * 256], U8, name="xs", tag="xs", align_bytes=64)
+            codes[b] = (xc, xs)
 
-        def quantise(n, part):
-            if part == 0:
-                xc = work.tile([P, 1024], U32, name="xc", tag="xc", align_bytes=64)
-                xs = work.tile([P, 1024], U8, name="xs", tag="xs", align_bytes=64)
-                codes[n] = (xc, xs)
-            xc, xs = codes[n]
-            cols = slice(part * 512, (part + 1) * 512)
+        def pieces(b):
+            size = len(bunches[b])
+            return {1: [(0, 1)], 2: [(0, 2)], 3: [(0, 2), (2, 3)], 4: [(0, 2), (2, 4)]}[size]
+
+        def quantise(b, piece):
+            lo, hi = piece
+            xc, xs = codes[b]
             nc.vector.quantize_mx(
-                out=xc[:, cols].bitcast(FP8X4), scales=xs[:, cols], in_=groups[n][:, part * 2048 : (part + 1) * 2048]
+                out=xc[:, lo * 256 : hi * 256].bitcast(FP8X4),
+                scales=xs[:, lo * 256 : hi * 256],
+                in_=groups[b][:, lo * 1024 : hi * 1024],
             )
 
-        def passes(n, i):
-            s, h = divmod(n, 2)
-            if h == 0 and i == 0:
+        def store(s, j0, j1):
+            nc.sync.dma_start(out=ov[s][:, j0 * D_OUT : j1 * D_OUT], in_=o_tiles[s][:, j0 * D_OUT : j1 * D_OUT])
+
+        def passes(b, i):
+            rt = bunches[b][i]
+            s, j = divmod(rt, J)
+            if j == 0:
                 o_slab = slabs.tile([P, J * D_OUT], F32, name="o_slab", tag="slab")
                 o_tiles[s] = o_slab
-            xc, xs = codes[n]
+            xc, xs = codes[b]
             ob = ps_o.tile([P, D_OUT], F32, name="ob", tag="O")
             for g in range(2):
                 m_cols = slice((2 * i + g) * P, (2 * i + g + 1) * P)
@@ -147,11 +163,16 @@ def tile_loralinear_t_kernel(tc, x, weight, bias, lora_left, lora_right, out):
                     start=(g == 0),
                     stop=(g == 1),
                 )
-            j = 4 * h + i
             nc.vector.tensor_tensor(out=o_tiles[s][:, j * D_OUT : (j + 1) * D_OUT], in0=ob[:], in1=bias_sb[:], op=ADD)
-
-        def store(s, j0, j1):
-            nc.sync.dma_start(out=ov[s][:, j0 * D_OUT : j1 * D_OUT], in_=o_tiles[s][:, j0 * D_OUT : j1 * D_OUT])
+            if s < SLABS - 1:
+                if j == J - 1:
+                    store(s, 0, J)
+            elif j == 3:
+                store(s, 0, 4)
+            elif j == 5:
+                store(s, 4, 6)
+            elif j == 7:
+                store(s, 6, 8)
 
         for t in range(4):
             weight_bank(0, t, True)
@@ -161,29 +182,18 @@ def tile_loralinear_t_kernel(tc, x, weight, bias, lora_left, lora_right, out):
         weight_bank(1, 1, True)
         weight_bank(1, 2, False)
         weight_bank(1, 3, False)
-        quantise(0, 0)
-        quantise(0, 1)
+        for piece in pieces(0):
+            quantise(0, piece)
         weight_quantise(1)
         transposes(1)
 
-        for n in range(UNITS):
-            s, h = divmod(n, 2)
-            last = s == SLABS - 1
-            if n + 1 < UNITS:
-                quantise(n + 1, 0)
-            passes(n, 0)
-            if n + 1 < UNITS:
-                quantise(n + 1, 1)
-            passes(n, 1)
-            if last and h == 1:
-                store(s, 4, 6)
-            passes(n, 2)
-            passes(n, 3)
-            if last and h == 0:
-                store(s, 0, 4)
-            elif last:
-                store(s, 6, 8)
-            elif h == 1:
-                store(s, 0, 8)
-            if n + 2 < UNITS:
-                transposes(n + 2)
+        for b in range(len(bunches)):
+            todo = pieces(b + 1) if b + 1 < len(bunches) else []
+            if todo:
+                quantise(b + 1, todo[0])
+            for i in range(len(bunches[b])):
+                passes(b, i)
+                if i + 1 < len(todo):
+                    quantise(b + 1, todo[i + 1])
+            if b + 2 < len(bunches):
+                transposes(b + 2)

@@ -18,8 +18,9 @@ RANK = 128
 LORA_SCALE = 2.0
 J = 8
 SLABS = ROWS // (P * J)
-BUNCH_SIZES = [2] * 32
-MAX_BUNCH = 2
+BUNCH_SIZES = [4] * 16
+MAX_BUNCH = 4
+GP_TILES = (0,)
 FLOPS = 2 * ROWS * D_IN * D_OUT + 2 * D_OUT * RANK * D_IN
 
 
@@ -30,7 +31,7 @@ def tile_loralinear_t_kernel(tc, x, weight, bias, lora_left, lora_right, out):
     with ExitStack() as ctx:
         const = ctx.enter_context(tc.tile_pool(name="const", bufs=1))
         slabs = ctx.enter_context(tc.tile_pool(name="slabs", bufs=9))
-        work = ctx.enter_context(tc.tile_pool(name="work", bufs=4))
+        work = ctx.enter_context(tc.tile_pool(name="work", bufs=3))
         ps_t = ctx.enter_context(tc.psum_pool(name="ps_t", bufs=4))
         ps_o = ctx.enter_context(tc.psum_pool(name="ps_o", bufs=4))
         ctx.enter_context(tc.manual_schedule())
@@ -163,7 +164,12 @@ def tile_loralinear_t_kernel(tc, x, weight, bias, lora_left, lora_right, out):
                     start=(g == 0),
                     stop=(g == 1),
                 )
-            nc.vector.tensor_tensor(out=o_tiles[s][:, j * D_OUT : (j + 1) * D_OUT], in0=ob[:], in1=bias_sb[:], op=ADD)
+            o_cols = o_tiles[s][:, j * D_OUT : (j + 1) * D_OUT]
+            if i in GP_TILES:
+                nc.scalar.copy(out=o_cols, in_=ob[:])
+                nc.gpsimd.tensor_tensor(out=o_cols, in0=o_cols, in1=bias_sb[:], op=ADD)
+            else:
+                nc.vector.tensor_tensor(out=o_cols, in0=ob[:], in1=bias_sb[:], op=ADD)
             if s < SLABS - 1:
                 if j == J - 1:
                     store(s, 0, J)

@@ -18,9 +18,9 @@ RANK = 128
 LORA_SCALE = 2.0
 J = 8
 SLABS = ROWS // (P * J)
-BUNCH_SIZES = [4] * 16
-MAX_BUNCH = 4
-GP_TILES = (0,)
+BUNCH_SIZES = [4, 4] + [8] * 7
+MAX_BUNCH = 8
+GP_EVERY = 4
 FLOPS = 2 * ROWS * D_IN * D_OUT + 2 * D_OUT * RANK * D_IN
 
 
@@ -31,9 +31,8 @@ def tile_loralinear_t_kernel(tc, x, weight, bias, lora_left, lora_right, out):
     with ExitStack() as ctx:
         const = ctx.enter_context(tc.tile_pool(name="const", bufs=1))
         slabs = ctx.enter_context(tc.tile_pool(name="slabs", bufs=9))
-        work = ctx.enter_context(tc.tile_pool(name="work", bufs=3))
-        ps_t = ctx.enter_context(tc.psum_pool(name="ps_t", bufs=4))
-        ps_o = ctx.enter_context(tc.psum_pool(name="ps_o", bufs=4))
+        work = ctx.enter_context(tc.tile_pool(name="work", bufs=2))
+        psum = ctx.enter_context(tc.psum_pool(name="psum", bufs=8))
         ctx.enter_context(tc.manual_schedule())
 
         ident_bf = const.tile([P, P], BF16, name="ident_bf")
@@ -64,13 +63,13 @@ def tile_loralinear_t_kernel(tc, x, weight, bias, lora_left, lora_right, out):
         for s in range(1, SLABS):
             nc.sync.dma_start(out=x_tiles[s][:], in_=xv[s])
 
-        pl = ps_t.tile([P, 4, P], BF16, name="pl", tag="T")
+        pl = psum.tile([P, 4, P], BF16, name="pl", tag="bank")
         for t in range(4):
             nc.tensor.transpose(pl[:, t, :], ll_sb[:, t, :], ident_bf[:])
         ll_t2 = const.tile([P, D_OUT], BF16, name="ll_t2")
         nc.vector.tensor_scalar_mul(out=ll_t2[:], in0=pl[:].rearrange("p t o -> p (t o)"), scalar1=LORA_SCALE)
 
-        pb = ps_t.tile([P, D_OUT], F32, name="pb", tag="T")
+        pb = psum.tile([P, D_OUT], F32, name="pb", tag="bank")
         nc.tensor.matmul(pb[:], lhsT=ones[:], rhs=bias_row[:], start=True, stop=True)
         bias_sb = const.tile([P, D_OUT], F32, name="bias_sb")
         nc.scalar.copy(out=bias_sb[:], in_=pb[:])
@@ -82,7 +81,7 @@ def tile_loralinear_t_kernel(tc, x, weight, bias, lora_left, lora_right, out):
         ws = const.tile([P, 2 * D_OUT], U8, name="ws", align_bytes=64)
 
         def weight_bank(g, t, on_vector):
-            pw = ps_o.tile([P, 4, P], F32, name="pw", tag="O")
+            pw = psum.tile([P, 4, P], F32, name="pw", tag="bank")
             for v in range(4):
                 u, e = divmod(v, 2)
                 nc.tensor.matmul(pw[:, v, :], lhsT=w_view[:, g, t, u, :, e], rhs=ident_bf[:], start=True, stop=False)
@@ -119,7 +118,7 @@ def tile_loralinear_t_kernel(tc, x, weight, bias, lora_left, lora_right, out):
             for i, rt in enumerate(tiles):
                 s, j = divmod(rt, J)
                 xw = x_tiles[s][:].bitcast(F32)
-                tb = ps_t.tile([P, 4, P], F32, name="tb", tag="T")
+                tb = psum.tile([P, 4, P], F32, name="tb", tag="bank")
                 for c in range(4):
                     nc.tensor.transpose(tb[:, c, :], xw[:, j * 512 + c * P : j * 512 + (c + 1) * P], ident_f[:])
                 nc.scalar.copy(out=gw[:, i], in_=tb[:].rearrange("p (g u) r -> p g r u", u=2))
@@ -130,7 +129,7 @@ def tile_loralinear_t_kernel(tc, x, weight, bias, lora_left, lora_right, out):
 
         def pieces(b):
             size = len(bunches[b])
-            return {1: [(0, 1)], 2: [(0, 2)], 3: [(0, 2), (2, 3)], 4: [(0, 2), (2, 4)]}[size]
+            return [(lo, lo + 2) for lo in range(0, size, 2)]
 
         def quantise(b, piece):
             lo, hi = piece
@@ -151,7 +150,7 @@ def tile_loralinear_t_kernel(tc, x, weight, bias, lora_left, lora_right, out):
                 o_slab = slabs.tile([P, J * D_OUT], F32, name="o_slab", tag="slab")
                 o_tiles[s] = o_slab
             xc, xs = codes[b]
-            ob = ps_o.tile([P, D_OUT], F32, name="ob", tag="O")
+            ob = psum.tile([P, D_OUT], F32, name="ob", tag="bank")
             for g in range(2):
                 m_cols = slice((2 * i + g) * P, (2 * i + g + 1) * P)
                 n_cols = slice(g * D_OUT, (g + 1) * D_OUT)
@@ -165,7 +164,7 @@ def tile_loralinear_t_kernel(tc, x, weight, bias, lora_left, lora_right, out):
                     stop=(g == 1),
                 )
             o_cols = o_tiles[s][:, j * D_OUT : (j + 1) * D_OUT]
-            if i in GP_TILES:
+            if j % GP_EVERY == 0:
                 nc.scalar.copy(out=o_cols, in_=ob[:])
                 nc.gpsimd.tensor_tensor(out=o_cols, in0=o_cols, in1=bias_sb[:], op=ADD)
             else:

@@ -20,6 +20,8 @@ J = 8
 SLABS = ROWS // (P * J)
 BUNCH_SIZES = [4, 4] + [8] * 7
 MAX_BUNCH = 8
+FINE_SLABS = 2
+WARM_UP = 4
 GP_EVERY = 4
 FLOPS = 2 * ROWS * D_IN * D_OUT + 2 * D_OUT * RANK * D_IN
 
@@ -41,8 +43,13 @@ def tile_loralinear_t_kernel(tc, x, weight, bias, lora_left, lora_right, out):
         masks.make_identity(nc, ident_f[:])
         ones = const.tile([P, P], BF16, name="ones")
         nc.vector.memset(ones[:], 1.0)
+        warm = const.tile([P, D_OUT], BF16, name="warm")
+        nc.vector.memset(warm[:], 0.0)
         bias_row = const.tile([P, D_OUT], BF16, name="bias_row")
         nc.vector.memset(bias_row[:], 0.0)
+        pd = psum.tile([P, D_OUT], F32, name="pd", tag="bank")
+        for n in range(WARM_UP):
+            nc.tensor.matmul(pd[:], lhsT=ones[:], rhs=warm[:], start=True, stop=True)
 
         ll_sb = const.tile([P, 4, RANK], BF16, name="ll_sb")
         nc.sync.dma_start(out=ll_sb[:], in_=lora_left.rearrange("(t p) r -> p t r", p=P))
@@ -56,7 +63,8 @@ def tile_loralinear_t_kernel(tc, x, weight, bias, lora_left, lora_right, out):
             x_slab = slabs.tile([P, J * D_IN], BF16, name="x_slab", tag="slab")
             x_tiles.append(x_slab)
         half = J * D_IN // 2
-        nc.sync.dma_start(out=w_sb[:, 0], in_=w_dram[0])
+        for t in range(4):
+            nc.sync.dma_start(out=w_sb[:, 0, t], in_=w_dram[0][:, t])
         nc.sync.dma_start(out=x_tiles[0][:, 0:half], in_=xv[0][:, 0:half])
         nc.sync.dma_start(out=w_sb[:, 1], in_=w_dram[1])
         nc.sync.dma_start(out=x_tiles[0][:, half : 2 * half], in_=xv[0][:, half : 2 * half])
@@ -69,10 +77,7 @@ def tile_loralinear_t_kernel(tc, x, weight, bias, lora_left, lora_right, out):
         ll_t2 = const.tile([P, D_OUT], BF16, name="ll_t2")
         nc.vector.tensor_scalar_mul(out=ll_t2[:], in0=pl[:].rearrange("p t o -> p (t o)"), scalar1=LORA_SCALE)
 
-        pb = psum.tile([P, D_OUT], F32, name="pb", tag="bank")
-        nc.tensor.matmul(pb[:], lhsT=ones[:], rhs=bias_row[:], start=True, stop=True)
         bias_sb = const.tile([P, D_OUT], F32, name="bias_sb")
-        nc.scalar.copy(out=bias_sb[:], in_=pb[:])
 
         w_view = w_sb[:].rearrange("p g t (u q e) -> p g t u q e", u=2, q=P, e=2)
         lr_view = lr_sb[:].rearrange("p (g u q e) -> p g u q e", g=2, u=2, q=P, e=2)
@@ -169,15 +174,9 @@ def tile_loralinear_t_kernel(tc, x, weight, bias, lora_left, lora_right, out):
                 nc.gpsimd.tensor_tensor(out=o_cols, in0=o_cols, in1=bias_sb[:], op=ADD)
             else:
                 nc.vector.tensor_tensor(out=o_cols, in0=ob[:], in1=bias_sb[:], op=ADD)
-            if s < SLABS - 1:
-                if j == J - 1:
-                    store(s, 0, J)
-            elif j == 3:
-                store(s, 0, 4)
-            elif j == 5:
-                store(s, 4, 6)
-            elif j == 7:
-                store(s, 6, 8)
+            step = J if s < SLABS - FINE_SLABS else 2
+            if (j + 1) % step == 0:
+                store(s, j + 1 - step, j + 1)
 
         for t in range(4):
             weight_bank(0, t, True)
@@ -190,6 +189,9 @@ def tile_loralinear_t_kernel(tc, x, weight, bias, lora_left, lora_right, out):
         for piece in pieces(0):
             quantise(0, piece)
         weight_quantise(1)
+        pb = psum.tile([P, D_OUT], F32, name="pb", tag="bank")
+        nc.tensor.matmul(pb[:], lhsT=ones[:], rhs=bias_row[:], start=True, stop=True)
+        nc.scalar.copy(out=bias_sb[:], in_=pb[:])
         transposes(1)
 
         for b in range(len(bunches)):

@@ -18,9 +18,9 @@ RANK = 128
 LORA_SCALE = 2.0
 J = 8
 SLABS = ROWS // (P * J)
-BUNCH_SIZES = [4, 4] + [8] * 7
-MAX_BUNCH = 8
-FINE_SLABS = 2
+BUNCH_SIZES = [4, 4, 8] + [12] * 4
+MAX_BUNCH = 12
+FINE_SLABS = 3
 WARM_UP = 4
 GP_EVERY = 4
 FLOPS = 2 * ROWS * D_IN * D_OUT + 2 * D_OUT * RANK * D_IN
@@ -32,7 +32,7 @@ def tile_loralinear_t_kernel(tc, x, weight, bias, lora_left, lora_right, out):
     ov = out.flatten_outer_dims().rearrange("(s p j) o -> s p (j o)", p=P, j=J)
     with ExitStack() as ctx:
         const = ctx.enter_context(tc.tile_pool(name="const", bufs=1))
-        slabs = ctx.enter_context(tc.tile_pool(name="slabs", bufs=9))
+        slabs = ctx.enter_context(tc.tile_pool(name="slabs", bufs=8))
         work = ctx.enter_context(tc.tile_pool(name="work", bufs=2))
         psum = ctx.enter_context(tc.psum_pool(name="psum", bufs=8))
         ctx.enter_context(tc.manual_schedule())
@@ -196,11 +196,16 @@ def tile_loralinear_t_kernel(tc, x, weight, bias, lora_left, lora_right, out):
 
         for b in range(len(bunches)):
             todo = pieces(b + 1) if b + 1 < len(bunches) else []
-            if todo:
-                quantise(b + 1, todo[0])
+            lead = (len(todo) + 1) // 2
+            for piece in todo[:lead]:
+                quantise(b + 1, piece)
+            rest = todo[lead:]
             for i in range(len(bunches[b])):
                 passes(b, i)
-                if i + 1 < len(todo):
-                    quantise(b + 1, todo[i + 1])
+                if i % 2 == 1 and rest:
+                    quantise(b + 1, rest[0])
+                    rest = rest[1:]
+            for piece in rest:
+                quantise(b + 1, piece)
             if b + 2 < len(bunches):
                 transposes(b + 2)

@@ -124,6 +124,12 @@ def tile_loralinear_t_kernel(tc, x, weight, bias, lora_left, lora_right, out):
                 s, j = divmod(rt, J)
                 xw = x_tiles[s][:].bitcast(F32)
                 tb = psum.tile([P, 4, P], F32, name="tb", tag="bank")
+                if len(tiles) >= 8 and (i == 0 or i == len(tiles) - 1):
+                    nc.tensor.matmul(
+                        tb[:, 0:2, :].rearrange("p a r -> p (a r)"), lhsT=ones[:], rhs=warm[:, 0 : 2 * P], start=True, stop=True
+                    )
+                elif len(tiles) >= 8 and i % 2 == 0:
+                    nc.tensor.matmul(tb[:, 0, :], lhsT=ones[:], rhs=warm[:, 0:P], start=True, stop=True)
                 for c in range(4):
                     nc.tensor.transpose(tb[:, c, :], xw[:, j * 512 + c * P : j * 512 + (c + 1) * P], ident_f[:])
                 nc.scalar.copy(out=gw[:, i], in_=tb[:].rearrange("p (g u) r -> p g r u", u=2))

from contextlib import ExitStack

import concourse.masks as masks
import concourse.mybir as mybir

F32 = mybir.dt.float32
BF16 = mybir.dt.bfloat16
U32 = mybir.dt.uint32
U8 = mybir.dt.uint8
FP8X4 = mybir.dt.float8_e4m3fn_x4
ADD = mybir.AluOpType.add

P = 128
ROWS = 8192
D_IN = 1024
D_OUT = 512
RANK = 128
LORA_SCALE = 2.0
J = 8
SLABS = ROWS // (P * J)
BUNCH_SIZES = [4, 4, 8] + [12] * 4
MAX_BUNCH = 12
FINE_SLABS = 3
WARM_UP = 4
GP_EVERY = 4
FLOPS = 2 * ROWS * D_IN * D_OUT + 2 * D_OUT * RANK * D_IN


def tile_loralinear_t_kernel(tc, x, weight, bias, lora_left, lora_right, out):
    nc = tc.nc
    xv = x.flatten_outer_dims().rearrange("(s p j) k -> s p (j k)", p=P, j=J)
    ov = out.flatten_outer_dims().rearrange("(s p j) o -> s p (j o)", p=P, j=J)
    with ExitStack() as ctx:
        const = ctx.enter_context(tc.tile_pool(name="const", bufs=1))
        slabs = ctx.enter_context(tc.tile_pool(name="slabs", bufs=8))
        work = ctx.enter_context(tc.tile_pool(name="work", bufs=2))
        psum = ctx.enter_context(tc.psum_pool(name="psum", bufs=8))
        ctx.enter_context(tc.manual_schedule())

        ident_bf = const.tile([P, P], BF16, name="ident_bf")
        masks.make_identity(nc, ident_bf[:])
        ident_f = const.tile([P, P], F32, name="ident_f")
        masks.make_identity(nc, ident_f[:])
        ones = const.tile([P, P], BF16, name="ones")
        nc.vector.memset(ones[:], 1.0)
        warm = const.tile([P, D_OUT], BF16, name="warm")
        nc.vector.memset(warm[:], 0.0)
        bias_row = const.tile([P, D_OUT], BF16, name="bias_row")
        nc.vector.memset(bias_row[:], 0.0)
        pd = psum.tile([P, D_OUT], F32, name="pd", tag="bank")
        for n in range(WARM_UP):
            nc.tensor.matmul(pd[:], lhsT=ones[:], rhs=warm[:], start=True, stop=True)

        ll_sb = const.tile([P, 4, RANK], BF16, name="ll_sb")
        nc.sync.dma_start(out=ll_sb[:], in_=lora_left.rearrange("(t p) r -> p t r", p=P))
        lr_sb = const.tile([P, D_IN], BF16, name="lr_sb")
        nc.sync.dma_start(out=lr_sb[:], in_=lora_right)
        nc.sync.dma_start(out=bias_row[0:1, :], in_=bias.unsqueeze(0))
        w_sb = const.tile([P, 2, 4, 512], BF16, name="w_sb")
        w_dram = weight.rearrange("(t p) (g k) -> g p t k", p=P, g=2)
        x_tiles = []
        for s in range(SLABS):
            x_slab = slabs.tile([P, J * D_IN], BF16, name="x_slab", tag="slab")
            x_tiles.append(x_slab)
        half = J * D_IN // 2
        for t in range(4):
            nc.sync.dma_start(out=w_sb[:, 0, t], in_=w_dram[0][:, t])
        nc.sync.dma_start(out=x_tiles[0][:, 0:half], in_=xv[0][:, 0:half])
        nc.sync.dma_start(out=w_sb[:, 1], in_=w_dram[1])
        nc.sync.dma_start(out=x_tiles[0][:, half : 2 * half], in_=xv[0][:, half : 2 * half])
        for s in range(1, SLABS):
            nc.sync.dma_start(out=x_tiles[s][:], in_=xv[s])

        pl = psum.tile([P, 4, P], BF16, name="pl", tag="bank")
        for t in range(4):
            nc.tensor.transpose(pl[:, t, :], ll_sb[:, t, :], ident_bf[:])
        ll_t2 = const.tile([P, D_OUT], BF16, name="ll_t2")
        nc.vector.tensor_scalar_mul(out=ll_t2[:], in0=pl[:].rearrange("p t o -> p (t o)"), scalar1=LORA_SCALE)

        bias_sb = const.tile([P, D_OUT], F32, name="bias_sb")

        w_view = w_sb[:].rearrange("p g t (u q e) -> p g t u q e", u=2, q=P, e=2)
        lr_view = lr_sb[:].rearrange("p (g u q e) -> p g u q e", g=2, u=2, q=P, e=2)
        wg = const.tile([P, 2, D_OUT, 4], BF16, name="wg", align_bytes=64)
        wc = const.tile([P, 2 * D_OUT], U32, name="wc", align_bytes=64)
        ws = const.tile([P, 2 * D_OUT], U8, name="ws", align_bytes=64)

        def weight_bank(g, t, on_vector):
            pw = psum.tile([P, 4, P], F32, name="pw", tag="bank")
            for v in range(4):
                u, e = divmod(v, 2)
                nc.tensor.matmul(pw[:, v, :], lhsT=w_view[:, g, t, u, :, e], rhs=ident_bf[:], start=True, stop=False)
                nc.tensor.matmul(
                    pw[:, v, :], lhsT=lr_view[:, g, u, :, e], rhs=ll_t2[:, t * P : (t + 1) * P], start=False, stop=True
                )
            dst = wg[:, g, t * P : (t + 1) * P, :]
            src = pw[:].rearrange("p v o -> p o v")
            if on_vector:
                nc.vector.tensor_copy(out=dst, in_=src)
            else:
                nc.scalar.copy(out=dst, in_=src)

        def weight_quantise(g):
            cols = slice(g * D_OUT, (g + 1) * D_OUT)
            nc.vector.quantize_mx(
                out=wc[:, cols].bitcast(FP8X4), scales=ws[:, cols], in_=wg[:, g].rearrange("p o v -> p (o v)")
            )

        bunches = []
        first = 0
        for size in BUNCH_SIZES:
            bunches.append(list(range(first, first + size)))
            first += size
        assert first == ROWS // P
        groups = {}
        codes = {}
        o_tiles = {}

        def transposes(b):
            tiles = bunches[b]
            grp = work.tile([P, MAX_BUNCH * 1024], BF16, name="grp", tag="grp", align_bytes=64)
            gw = grp[:].bitcast(F32).rearrange("p (i g r u) -> p i g r u", i=MAX_BUNCH, g=2, r=P, u=2)
            for i, rt in enumerate(tiles):
                s, j = divmod(rt, J)
                xw = x_tiles[s][:].bitcast(F32)
                tb = psum.tile([P, 4, P], F32, name="tb", tag="bank")
                if len(tiles) >= 8 and (i == 0 or i == len(tiles) - 1):
                    nc.tensor.matmul(
                        tb[:, 0:2, :].rearrange("p a r -> p (a r)"), lhsT=ones[:], rhs=warm[:, 0 : 2 * P], start=True, stop=True
                    )
                elif len(tiles) >= 8 and i % 2 == 0:
                    nc.tensor.matmul(tb[:, 0, :], lhsT=ones[:], rhs=warm[:, 0:P], start=True, stop=True)
                for c in range(4):
                    nc.tensor.transpose(tb[:, c, :], xw[:, j * 512 + c * P : j * 512 + (c + 1) * P], ident_f[:])
                nc.scalar.copy(out=gw[:, i], in_=tb[:].rearrange("p (g u) r -> p g r u", u=2))
            groups[b] = grp
            xc = work.tile([P, MAX_BUNCH * 256], U32, name="xc", tag="xc", align_bytes=64)
            xs = work.tile([P, MAX_BUNCH * 256], U8, name="xs", tag="xs", align_bytes=64)
            codes[b] = (xc, xs)

        def pieces(b):
            size = len(bunches[b])
            return [(lo, lo + 2) for lo in range(0, size, 2)]

        def quantise(b, piece):
            lo, hi = piece
            xc, xs = codes[b]
            nc.vector.quantize_mx(
                out=xc[:, lo * 256 : hi * 256].bitcast(FP8X4),
                scales=xs[:, lo * 256 : hi * 256],
                in_=groups[b][:, lo * 1024 : hi * 1024],
            )

        def store(s, j0, j1):
            nc.sync.dma_start(out=ov[s][:, j0 * D_OUT : j1 * D_OUT], in_=o_tiles[s][:, j0 * D_OUT : j1 * D_OUT])

        def passes(b, i):
            rt = bunches[b][i]
            s, j = divmod(rt, J)
            if j == 0:
                o_slab = slabs.tile([P, J * D_OUT], F32, name="o_slab", tag="slab")
                o_tiles[s] = o_slab
            xc, xs = codes[b]
            ob = psum.tile([P, D_OUT], F32, name="ob", tag="bank")
            for g in range(2):
                m_cols = slice((2 * i + g) * P, (2 * i + g + 1) * P)
                n_cols = slice(g * D_OUT, (g + 1) * D_OUT)
                nc.tensor.matmul_mx(
                    out=ob[:],
                    lhsT=xc[:, m_cols].bitcast(FP8X4),
                    lhsT_scale=xs[:, m_cols],
                    rhs=wc[:, n_cols].bitcast(FP8X4),
                    rhs_scale=ws[:, n_cols],
                    start=(g == 0),
                    stop=(g == 1),
                )
            o_cols = o_tiles[s][:, j * D_OUT : (j + 1) * D_OUT]
            if j % GP_EVERY == 0:
                nc.scalar.copy(out=o_cols, in_=ob[:])
                nc.gpsimd.tensor_tensor(out=o_cols, in0=o_cols, in1=bias_sb[:], op=ADD)
            else:
                nc.vector.tensor_tensor(out=o_cols, in0=ob[:], in1=bias_sb[:], op=ADD)
            step = J if s < SLABS - FINE_SLABS else 2
            if (j + 1) % step == 0:
                store(s, j + 1 - step, j + 1)

        for t in range(4):
            weight_bank(0, t, True)
        weight_quantise(0)
        transposes(0)
        weight_bank(1, 0, True)
        weight_bank(1, 1, True)
        weight_bank(1, 2, False)
        weight_bank(1, 3, False)
        for piece in pieces(0):
            quantise(0, piece)
        weight_quantise(1)
        pb = psum.tile([P, D_OUT], F32, name="pb", tag="bank")
        nc.tensor.matmul(pb[:], lhsT=ones[:], rhs=bias_row[:], start=True, stop=True)
        nc.scalar.copy(out=bias_sb[:], in_=pb[:])
        transposes(1)

        for b in range(len(bunches)):
            todo = pieces(b + 1) if b + 1 < len(bunches) else []
            lead = (len(todo) + 1) // 2
            for piece in todo[:lead]:
                quantise(b + 1, piece)
            rest = todo[lead:]
            for i in range(len(bunches[b])):
                passes(b, i)
                if i % 2 == 1 and rest:
                    quantise(b + 1, rest[0])
                    rest = rest[1:]
            for piece in rest:
                quantise(b + 1, piece)
            if b + 2 < len(bunches):
                transposes(b + 2)
